import numpy as np
import ml_dtypes


def mxq(x, axis, fmt="e4m3"):
    dtype, down = {"e4m3": (ml_dtypes.float8_e4m3fn, 7), "e5m2": (ml_dtypes.float8_e5m2, 14)}[fmt]
    v = np.moveaxis(np.asarray(x, np.float32).astype(ml_dtypes.bfloat16).astype(np.float64), axis, -1)
    blocks = v.reshape(v.shape[:-1] + (-1, 32))
    amax = np.abs(blocks).max(-1, keepdims=True)
    byte = np.maximum(np.where(amax > 0, np.frexp(amax)[1] - 1 + 127, 0) - down, 1)
    scale = np.exp2(byte - 127.0)
    codes = (blocks / scale).astype(np.float32).astype(dtype).astype(np.float64)
    return np.moveaxis((codes * scale).reshape(v.shape), -1, axis)


WIDE = False


def mx_kscale(k):
    if not WIDE:
        return np.ones(k)
    levels = np.array([10, -10, 5, -5, 0])
    if k % 512:
        return np.exp2(np.random.permutation(np.resize(levels, k // 32))).repeat(32)
    a = np.empty((k // 512, 16))
    for p in range(k // 512):
        a[p, :8] = np.random.permutation(np.resize(levels, 8))
        for g in range(8):
            far = levels[np.abs(levels - a[p, g]) >= 10]
            a[p, g + 8] = far[np.random.randint(len(far))]
    return np.exp2(a.ravel()).repeat(32)


BF16 = ml_dtypes.bfloat16


def bf(x):
    return np.asarray(x, np.float32).astype(BF16)


def f64(x):
    return np.asarray(x).astype(np.float64)


B, N, D = 16, 256, 1024


def setup_inputs():
    s = mx_kscale(D)
    return {"column_embeddings": bf(np.random.standard_normal((B, N, D)) / D**0.25 * s),
            "W": bf(np.random.uniform(-1.0, 1.0, (D, D)) * np.sqrt(3.0 / D) / s[:, None] / s[None, :]),
            "b": bf(0.3 + 0.1 * np.random.standard_normal(1))}


def reference(column_embeddings, W, b):
    xq = mxq(f64(column_embeddings), 2, "e4m3")
    xw = xq @ mxq(f64(W), 0, "e4m3")
    scores = (mxq(xw, 2, "e4m3") @ xq.transpose(0, 2, 1)) + f64(b)
    corr = np.tanh(scores)
    eye = np.eye(column_embeddings.shape[1], dtype=bool)
    return np.where(eye[None, :, :], 1.0, corr)

@@ -1,0 +1,357 @@
+from contextlib import ExitStack
+
+import concourse.mybir as mybir
+from concourse.masks import make_identity
+
+F32 = mybir.dt.float32
+BF16 = mybir.dt.bfloat16
+I32 = mybir.dt.int32
+U32 = mybir.dt.uint32
+U8 = mybir.dt.uint8
+FP8X4 = mybir.dt.float8_e4m3fn_x4
+ACT = mybir.ActivationFunctionType
+ALU = mybir.AluOpType
+
+P = 128
+BATCHES, ROWS, FEATURES = 16, 256, 1024
+PASS = 512
+PASSES = FEATURES // PASS
+GROUPS = 4
+BLOCKS = ROWS // P
+FLOPS = 2 * BATCHES * ROWS * FEATURES * FEATURES + 2 * BATCHES * ROWS * ROWS * FEATURES
+
+VECTOR, SCALAR = "vector", "scalar"
+
+QUANTISED_ALONE = ((14, 1), (15, 1))
+
+
+def tile_columncorrelationhead_kernel(tc, column_embeddings, W, b, out):
+    nc = tc.nc
+    x_rows = column_embeddings.flatten_outer_dims().rearrange("(c p) d -> p c d", p=P)
+    out_rows = out.flatten_outer_dims().rearrange("(c p) j -> p c j", p=P)
+    w_view = W.rearrange("(g p t) c -> p g t c", g=PASSES, p=P, t=4)
+
+    with ExitStack() as ctx:
+        ctx.enter_context(tc.manual_schedule())
+        keep = ctx.enter_context(tc.tile_pool(name="keep", bufs=1))
+        xg_pool = ctx.enter_context(tc.tile_pool(name="xg_pool", bufs=4))
+        xwg_pool = ctx.enter_context(tc.tile_pool(name="xwg_pool", bufs=4))
+        xwc_pool = ctx.enter_context(tc.tile_pool(name="xwc_pool", bufs=6))
+        solo_pool = ctx.enter_context(tc.tile_pool(name="solo_pool", bufs=2))
+        o_pool = ctx.enter_context(tc.tile_pool(name="o_pool", bufs=6))
+        psum = ctx.enter_context(tc.psum_pool(name="psum", bufs=8))
+
+        def copy(engine, dst, src):
+            if engine == VECTOR:
+                nc.vector.tensor_copy(out=dst, in_=src)
+            else:
+                nc.scalar.copy(out=dst, in_=src)
+
+        zero_codes = keep.tile([P, PASS], U32, name="zero_codes", align_bytes=64)
+        zero_scales = keep.tile([P, PASS], U8, name="zero_scales", align_bytes=64)
+        zeros = keep.tile([P, 4 * PASS], BF16, name="zeros", align_bytes=64)
+        nc.vector.memset(zeros[:].bitcast(I32), 0)
+        nc.vector.quantize_mx(out=zero_codes[:].bitcast(FP8X4), scales=zero_scales[:], in_=zeros[:])
+        ident = keep.tile([P, P], F32, name="ident")
+        make_identity(nc, ident[:])
+        diag_mask = keep.tile([P, P], F32, name="diag_mask")
+        nc.vector.tensor_scalar(out=diag_mask[:], in0=ident[:], scalar1=2.0, scalar2=-1.0,
+                                op0=ALU.mult, op1=ALU.add)
+        b_bf16 = keep.tile([P, 1], BF16, name="b_bf16")
+        nc.scalar.dma_start(out=b_bf16[:], in_=b.partition_broadcast(P))
+        table_load = keep.tile([P, 1], F32, name="table_load")
+        nc.scalar.activation(out=table_load[:], in_=ident[:, 0:1], func=ACT.Tanh)
+        bias = keep.tile([P, 1], F32, name="bias")
+
+        x_raw = [keep.tile([P, BLOCKS, FEATURES], BF16, name="x_raw%d" % n) for n in range(BATCHES)]
+        x_codes = [keep.tile([P, PASSES, ROWS], U32, name="x_codes%d" % n, align_bytes=64)
+                   for n in range(BATCHES)]
+        x_scales = [keep.tile([P, PASSES, ROWS], U8, name="x_scales%d" % n, align_bytes=64)
+                    for n in range(BATCHES)]
+        w_raw, w_words, w_codes, w_scales = {}, {}, {}, {}
+        for s in range(PASSES):
+            for g in range(PASSES):
+                w_raw[s, g] = keep.tile([P, 4, PASS], BF16, name="w_raw%d%d" % (s, g))
+                w_words[s, g] = keep.tile([P, 4 * PASS], BF16, name="w_words%d%d" % (s, g),
+                                          align_bytes=64)
+                w_codes[s, g] = keep.tile([P, PASS], U32, name="w_codes%d%d" % (s, g),
+                                          align_bytes=64)
+                w_scales[s, g] = keep.tile([P, PASS], U8, name="w_scales%d%d" % (s, g),
+                                           align_bytes=64)
+        live = {}
+
+        def load_x(n):
+            nc.sync.dma_start(out=x_raw[n][:], in_=x_rows[:, BLOCKS * n:BLOCKS * (n + 1), :])
+
+        def load_w(s, g):
+            nc.sync.dma_start(out=w_raw[s, g][:], in_=w_view[:, g, :, s * PASS:(s + 1) * PASS])
+
+        def warm_up(passes):
+            scratch = psum.tile([P, PASS], F32, name="bank", tag="bank")
+            for k in range(passes):
+                nc.tensor.matmul_mx(out=scratch[:], lhsT=zero_codes[:, 0:P].bitcast(FP8X4),
+                                    lhsT_scale=zero_scales[:, 0:P],
+                                    rhs=zero_codes[:].bitcast(FP8X4), rhs_scale=zero_scales[:],
+                                    start=True, stop=True)
+
+        def transposes(n):
+            pairs = x_raw[n][:].bitcast(F32)
+            for g in range(PASSES):
+                bank = psum.tile([P, 2, ROWS], F32, name="bank", tag="bank")
+                for u in range(2):
+                    for block in range(BLOCKS):
+                        lo = (PASS // 2) * g
+                        nc.tensor.transpose(bank[:, u, block * P:(block + 1) * P],
+                                            pairs[:, block, lo + u:lo + PASS // 2:2], ident[:])
+                live["xT", n, g] = bank
+            live["xg", n] = xg_pool.tile([P, PASSES, 4 * ROWS], BF16, name="xg", tag="xg",
+                                         align_bytes=64)
+
+        def copy_transposed(n, g, engine):
+            pairs = live["xg", n][:].bitcast(F32)
+            copy(engine, pairs[:, g, :].rearrange("p (i u) -> p i u", u=2),
+                 live["xT", n, g][:].rearrange("p u i -> p i u"))
+
+        def quantise_x(n):
+            nc.vector.quantize_mx(out=x_codes[n][:].rearrange("p g i -> p (g i)").bitcast(FP8X4),
+                                  scales=x_scales[n][:].rearrange("p g i -> p (g i)"),
+                                  in_=live["xg", n][:].rearrange("p g c -> p (g c)"))
+
+        def regroup_w(s, g, group, engine):
+            src = w_raw[s, g][:].rearrange("p t (q f) -> p f q t", f=GROUPS)[:, group]
+            dst = w_words[s, g][:].rearrange("p (f q t) -> p f q t", f=GROUPS, t=4)[:, group]
+            copy(engine, dst, src)
+
+        def quantise_w(s, g, first_group, groups):
+            words = slice(first_group * P, (first_group + groups) * P)
+            nc.vector.quantize_mx(out=w_codes[s, g][:, words].bitcast(FP8X4),
+                                  scales=w_scales[s, g][:, words],
+                                  in_=w_words[s, g][:, 4 * first_group * P:4 * (first_group + groups) * P])
+
+        def first_matmul_groups(n, s, block, groups):
+            bank = live["xwT", n, s, block]
+            rows = slice(block * P, (block + 1) * P)
+            for t in groups:
+                cols = slice(t * P, (t + 1) * P)
+                for g in range(PASSES):
+                    nc.tensor.matmul_mx(out=bank[:, cols],
+                                        lhsT=w_codes[s, g][:, cols].bitcast(FP8X4),
+                                        lhsT_scale=w_scales[s, g][:, cols],
+                                        rhs=x_codes[n][:, g, rows].bitcast(FP8X4),
+                                        rhs_scale=x_scales[n][:, g, rows],
+                                        start=(g == 0), stop=(g == PASSES - 1))
+
+        def first_matmul_open(n, s, block):
+            live["xwT", n, s, block] = psum.tile([P, PASS], F32, name="bank", tag="bank")
+            first_matmul_groups(n, s, block, (0, 1))
+
+        def xw_place(n, s):
+            if (n, s) in QUANTISED_ALONE:
+                return (n, s), 0, 1
+            return (n - n % 2, s), n % 2, 2
+
+        def first_matmul_close(n, s, block, engine):
+            first_matmul_groups(n, s, block, (2, 3))
+            key, place, batches = xw_place(n, s)
+            if ("xwg", key) not in live:
+                if batches == 1:
+                    live["xwg", key] = solo_pool.tile([P, ROWS, 4], BF16, name="xwg1", tag="xwg1",
+                                                      align_bytes=64)
+                else:
+                    live["xwg", key] = xwg_pool.tile([P, 2 * ROWS, 4], BF16, name="xwg", tag="xwg",
+                                                     align_bytes=64)
+            lo = (BLOCKS * place + block) * P
+            copy(engine, live["xwg", key][:, lo:lo + P, :],
+                 live["xwT", n, s, block][:].rearrange("p (t i) -> p i t", t=GROUPS))
+
+        def first_matmul(n, s, block, engine):
+            first_matmul_open(n, s, block)
+            first_matmul_close(n, s, block, engine)
+
+        def quantise_xw(n, s):
+            key, place, batches = xw_place(n, s)
+            if batches == 1:
+                codes = solo_pool.tile([P, ROWS], U32, name="xwc1", tag="xwc1", align_bytes=64)
+                scales = solo_pool.tile([P, ROWS], U8, name="xws1", tag="xws1", align_bytes=64)
+            else:
+                codes = xwc_pool.tile([P, 2 * ROWS], U32, name="xwc", tag="xwc", align_bytes=64)
+                scales = xwc_pool.tile([P, 2 * ROWS], U8, name="xws", tag="xws", align_bytes=64)
+            nc.vector.quantize_mx(out=codes[:].bitcast(FP8X4), scales=scales[:],
+                                  in_=live["xwg", key][:].rearrange("p i t -> p (i t)"))
+            live["xwc", key] = (codes, scales)
+
+        def second_matmul(n):
+            result = o_pool.tile([P, BLOCKS, ROWS], F32, name="o", tag="o")
+            live["o", n] = result
+            bank = psum.tile([P, PASS], F32, name="bank", tag="bank")
+            for block in range(BLOCKS):
+                for s in range(PASSES):
+                    key, place, batches = xw_place(n, s)
+                    codes, scales = live["xwc", key]
+                    rows = slice((BLOCKS * place + block) * P, (BLOCKS * place + block + 1) * P)
+                    nc.tensor.matmul_mx(out=bank[:, block * ROWS:(block + 1) * ROWS],
+                                        lhsT=codes[:, rows].bitcast(FP8X4),
+                                        lhsT_scale=scales[:, rows],
+                                        rhs=x_codes[n][:, s, :].bitcast(FP8X4),
+                                        rhs_scale=x_scales[n][:, s, :],
+                                        start=(s == 0), stop=(s == PASSES - 1))
+            nc.scalar.activation(out=result[:], in_=bank[:].rearrange("p (r j) -> p r j", r=BLOCKS),
+                                 func=ACT.Tanh, bias=bias[:, 0:1], scale=1.0)
+
+        def finish(n):
+            result = live["o", n]
+            diagonal = result[:].rearrange("p r (a k) -> p (r a) k", k=P)[:, 0:4:3, :]
+            nc.vector.tensor_tensor(out=diagonal, in0=diagonal,
+                                    in1=diag_mask[:].unsqueeze(1).to_broadcast([P, BLOCKS, P]),
+                                    op=ALU.max)
+            nc.sync.dma_start(out=out_rows[:, BLOCKS * n:BLOCKS * (n + 1), :], in_=result[:])
+
+        load_x(0)
+        load_w(0, 0)
+        load_w(0, 1)
+        for n in range(1, 6):
+            load_x(n)
+        load_w(1, 0)
+        load_w(1, 1)
+        for n in range(6, BATCHES):
+            load_x(n)
+
+        warm_up(6)
+        transposes(0)
+        for group, engine in ((0, VECTOR), (1, VECTOR), (2, VECTOR), (3, SCALAR)):
+            regroup_w(0, 0, group, engine)
+        copy_transposed(0, 0, SCALAR)
+        copy_transposed(0, 1, SCALAR)
+        warm_up(5)
+        quantise_w(0, 0, 0, 2)
+        quantise_w(0, 0, 2, 2)
+        regroup_w(0, 1, 0, SCALAR)
+        regroup_w(0, 1, 1, VECTOR)
+        quantise_x(0)
+        transposes(1)
+        quantise_w(0, 1, 0, 2)
+        regroup_w(0, 1, 2, VECTOR)
+        regroup_w(0, 1, 3, SCALAR)
+        copy_transposed(1, 0, SCALAR)
+        first_matmul_open(0, 0, 0)
+        first_matmul_open(0, 0, 1)
+        quantise_w(0, 1, 2, 2)
+        nc.vector.tensor_copy(out=bias[:], in_=b_bf16[:])
+        copy_transposed(1, 1, VECTOR)
+        quantise_x(1)
+        first_matmul_close(0, 0, 0, SCALAR)
+        first_matmul_close(0, 0, 1, VECTOR)
+
+        transposes(2)
+        copy_transposed(2, 0, SCALAR)
+        copy_transposed(2, 1, VECTOR)
+        quantise_x(2)
+        first_matmul(1, 0, 0, VECTOR)
+        first_matmul(1, 0, 1, VECTOR)
+        transposes(3)
+        first_matmul(2, 0, 0, SCALAR)
+        first_matmul(2, 0, 1, SCALAR)
+        copy_transposed(3, 0, VECTOR)
+        copy_transposed(3, 1, VECTOR)
+        transposes(4)
+        transposes(5)
+        copy_transposed(4, 1, SCALAR)
+        copy_transposed(5, 0, SCALAR)
+        quantise_x(3)
+        copy_transposed(5, 1, SCALAR)
+        first_matmul(3, 0, 0, SCALAR)
+        regroup_w(1, 0, 1, VECTOR)
+        regroup_w(1, 0, 0, SCALAR)
+        copy_transposed(4, 0, VECTOR)
+        quantise_x(4)
+        first_matmul(3, 0, 1, SCALAR)
+        regroup_w(1, 0, 2, VECTOR)
+        quantise_x(5)
+        first_matmul(4, 0, 0, SCALAR)
+        regroup_w(1, 0, 3, VECTOR)
+        first_matmul(4, 0, 1, SCALAR)
+        quantise_w(1, 0, 0, GROUPS)
+        regroup_w(1, 1, 0, VECTOR)
+        first_matmul(5, 0, 0, SCALAR)
+        first_matmul(5, 0, 1, SCALAR)
+        transposes(6)
+        transposes(7)
+        regroup_w(1, 1, 1, VECTOR)
+        regroup_w(1, 1, 2, VECTOR)
+        copy_transposed(6, 0, SCALAR)
+        regroup_w(1, 1, 3, VECTOR)
+        copy_transposed(7, 0, SCALAR)
+        quantise_w(1, 1, 0, GROUPS)
+        copy_transposed(7, 1, SCALAR)
+        copy_transposed(6, 1, VECTOR)
+
+        quantise_xw(0, 0)
+        first_matmul(0, 1, 0, VECTOR)
+        quantise_xw(2, 0)
+        first_matmul(0, 1, 1, SCALAR)
+        quantise_xw(4, 0)
+        first_matmul(1, 1, 0, SCALAR)
+        quantise_x(6)
+        first_matmul(1, 1, 1, SCALAR)
+        quantise_x(7)
+        for n in (2, 3):
+            for block in range(BLOCKS):
+                first_matmul(n, 1, block, SCALAR)
+        quantise_xw(0, 1)
+        second_matmul(0)
+        quantise_xw(2, 1)
+        second_matmul(1)
+        first_matmul(4, 1, 0, SCALAR)
+        first_matmul(4, 1, 1, SCALAR)
+        finish(0)
+        first_matmul(5, 1, 0, VECTOR)
+        first_matmul(5, 1, 1, SCALAR)
+        second_matmul(2)
+        quantise_xw(4, 1)
+        finish(1)
+        second_matmul(3)
+
+        def pass_0(a):
+            first_matmul(a, 0, 0, SCALAR)
+            first_matmul(a, 0, 1, SCALAR)
+            finish(a - 4)
+            first_matmul(a + 1, 0, 0, VECTOR)
+            finish(a - 3)
+            first_matmul(a + 1, 0, 1, SCALAR)
+
+        last = BATCHES - 2
+        for a in range(6, last, 2):
+            pass_0(a)
+            second_matmul(a - 2)
+            quantise_xw(a, 0)
+            second_matmul(a - 1)
+            transposes(a + 2)
+            transposes(a + 3)
+            copy_transposed(a + 2, 0, VECTOR)
+            copy_transposed(a + 2, 1, VECTOR)
+            copy_transposed(a + 3, 0, SCALAR)
+            copy_transposed(a + 3, 1, VECTOR)
+            quantise_x(a + 2)
+            first_matmul(a, 1, 0, SCALAR)
+            first_matmul(a, 1, 1, SCALAR)
+            quantise_x(a + 3)
+            first_matmul(a + 1, 1, 0, VECTOR)
+            first_matmul(a + 1, 1, 1, SCALAR)
+            quantise_xw(a, 1)
+
+        pass_0(last)
+        quantise_xw(last, 0)
+        first_matmul(last, 1, 0, SCALAR)
+        first_matmul(last, 1, 1, VECTOR)
+        first_matmul(last + 1, 1, 0, SCALAR)
+        quantise_xw(last, 1)
+        first_matmul(last + 1, 1, 1, VECTOR)
+        second_matmul(last - 2)
+        quantise_xw(last + 1, 1)
+        second_matmul(last - 1)
+        second_matmul(last)
+        finish(last - 2)
+        second_matmul(last + 1)
+        finish(last - 1)
+        finish(last)
+        finish(last + 1)

@@ -35,6 +35,7 @@ def tile_columncorrelationhead_kernel(tc, column_embeddings, W, b, out):
         ctx.enter_context(tc.manual_schedule())
         keep = ctx.enter_context(tc.tile_pool(name="keep", bufs=1))
         xg_pool = ctx.enter_context(tc.tile_pool(name="xg_pool", bufs=4))
+        xp_pool = ctx.enter_context(tc.tile_pool(name="xp_pool", bufs=5))
         xwg_pool = ctx.enter_context(tc.tile_pool(name="xwg_pool", bufs=4))
         xwc_pool = ctx.enter_context(tc.tile_pool(name="xwc_pool", bufs=6))
         solo_pool = ctx.enter_context(tc.tile_pool(name="solo_pool", bufs=2))
@@ -49,9 +50,12 @@ def tile_columncorrelationhead_kernel(tc, column_embeddings, W, b, out):
 
         zero_codes = keep.tile([P, PASS], U32, name="zero_codes", align_bytes=64)
         zero_scales = keep.tile([P, PASS], U8, name="zero_scales", align_bytes=64)
-        zeros = keep.tile([P, 4 * PASS], BF16, name="zeros", align_bytes=64)
+        zeros = keep.tile([P, 2 * PASS], BF16, name="zeros", align_bytes=64)
         nc.vector.memset(zeros[:].bitcast(I32), 0)
-        nc.vector.quantize_mx(out=zero_codes[:].bitcast(FP8X4), scales=zero_scales[:], in_=zeros[:])
+        for half in range(2):
+            cols = slice(half * PASS // 2, (half + 1) * PASS // 2)
+            nc.vector.quantize_mx(out=zero_codes[:, cols].bitcast(FP8X4),
+                                  scales=zero_scales[:, cols], in_=zeros[:])
         ident = keep.tile([P, P], F32, name="ident")
         make_identity(nc, ident[:])
         diag_mask = keep.tile([P, P], F32, name="diag_mask")
@@ -94,15 +98,27 @@ def tile_columncorrelationhead_kernel(tc, column_embeddings, W, b, out):
                                     rhs=zero_codes[:].bitcast(FP8X4), rhs_scale=zero_scales[:],
                                     start=True, stop=True)
 
+        def sort_pairs(n):
+            live["xp", n] = xp_pool.tile([P, BLOCKS, FEATURES], BF16, name="xp", tag="xp",
+                                         align_bytes=64)
+            src = x_raw[n][:].bitcast(F32).rearrange("p b (g i u) -> p (b g) u i", g=PASSES, u=2)
+            dst = live["xp", n][:].bitcast(F32).rearrange("p b (g u i) -> p (b g) u i", g=PASSES, u=2)
+            nc.vector.tensor_copy(out=dst, in_=src)
+
         def transposes(n):
-            pairs = x_raw[n][:].bitcast(F32)
+            is_sorted = ("xp", n) in live
+            pairs = (live["xp", n] if is_sorted else x_raw[n])[:].bitcast(F32)
             for g in range(PASSES):
                 bank = psum.tile([P, 2, ROWS], F32, name="bank", tag="bank")
                 for u in range(2):
                     for block in range(BLOCKS):
                         lo = (PASS // 2) * g
+                        if is_sorted:
+                            plane = slice(lo + u * P, lo + (u + 1) * P)
+                        else:
+                            plane = slice(lo + u, lo + PASS // 2, 2)
                         nc.tensor.transpose(bank[:, u, block * P:(block + 1) * P],
-                                            pairs[:, block, lo + u:lo + PASS // 2:2], ident[:])
+                                            pairs[:, block, plane], ident[:])
                 live["xT", n, g] = bank
             live["xg", n] = xg_pool.tile([P, PASSES, 4 * ROWS], BF16, name="xg", tag="xg",
                                          align_bytes=64)
@@ -310,6 +326,8 @@ def tile_columncorrelationhead_kernel(tc, column_embeddings, W, b, out):
         quantise_xw(4, 1)
         finish(1)
         second_matmul(3)
+        sort_pairs(8)
+        sort_pairs(9)
 
         def pass_0(a):
             first_matmul(a, 0, 0, SCALAR)
@@ -328,12 +346,15 @@ def tile_columncorrelationhead_kernel(tc, column_embeddings, W, b, out):
             transposes(a + 2)
             transposes(a + 3)
             copy_transposed(a + 2, 0, VECTOR)
-            copy_transposed(a + 2, 1, VECTOR)
+            copy_transposed(a + 2, 1, SCALAR)
             copy_transposed(a + 3, 0, SCALAR)
             copy_transposed(a + 3, 1, VECTOR)
             quantise_x(a + 2)
             first_matmul(a, 1, 0, SCALAR)
             first_matmul(a, 1, 1, SCALAR)
+            if a + 4 < BATCHES:
+                sort_pairs(a + 4)
+                sort_pairs(a + 5)
             quantise_x(a + 3)
             first_matmul(a + 1, 1, 0, VECTOR)
             first_matmul(a + 1, 1, 1, SCALAR)

@@ -87,6 +87,9 @@ def tile_columncorrelationhead_kernel(tc, column_embeddings, W, b, out):
         def load_x(n):
             nc.sync.dma_start(out=x_raw[n][:], in_=x_rows[:, BLOCKS * n:BLOCKS * (n + 1), :])
 
+        def load_x_block(n, block):
+            nc.sync.dma_start(out=x_raw[n][:, block, :], in_=x_rows[:, BLOCKS * n + block, :])
+
         def load_w(s, g):
             nc.sync.dma_start(out=w_raw[s, g][:], in_=w_view[:, g, :, s * PASS:(s + 1) * PASS])
 
@@ -98,35 +101,41 @@ def tile_columncorrelationhead_kernel(tc, column_embeddings, W, b, out):
                                     rhs=zero_codes[:].bitcast(FP8X4), rhs_scale=zero_scales[:],
                                     start=True, stop=True)
 
-        def sort_pairs(n):
+        def sort_pairs(n, engine):
             live["xp", n] = xp_pool.tile([P, BLOCKS, FEATURES], BF16, name="xp", tag="xp",
                                          align_bytes=64)
             src = x_raw[n][:].bitcast(F32).rearrange("p b (g i u) -> p (b g) u i", g=PASSES, u=2)
             dst = live["xp", n][:].bitcast(F32).rearrange("p b (g u i) -> p (b g) u i", g=PASSES, u=2)
-            nc.vector.tensor_copy(out=dst, in_=src)
+            copy(engine, dst, src)
 
-        def transposes(n):
+        def transposes(n, block):
             is_sorted = ("xp", n) in live
             pairs = (live["xp", n] if is_sorted else x_raw[n])[:].bitcast(F32)
+            bank = psum.tile([P, PASSES, 2, P], F32, name="bank", tag="bank")
             for g in range(PASSES):
-                bank = psum.tile([P, 2, ROWS], F32, name="bank", tag="bank")
                 for u in range(2):
-                    for block in range(BLOCKS):
-                        lo = (PASS // 2) * g
-                        if is_sorted:
-                            plane = slice(lo + u * P, lo + (u + 1) * P)
-                        else:
-                            plane = slice(lo + u, lo + PASS // 2, 2)
-                        nc.tensor.transpose(bank[:, u, block * P:(block + 1) * P],
-                                            pairs[:, block, plane], ident[:])
-                live["xT", n, g] = bank
-            live["xg", n] = xg_pool.tile([P, PASSES, 4 * ROWS], BF16, name="xg", tag="xg",
-                                         align_bytes=64)
+                    lo = (PASS // 2) * g
+                    if is_sorted:
+                        plane = slice(lo + u * P, lo + (u + 1) * P)
+                    else:
+                        plane = slice(lo + u, lo + PASS // 2, 2)
+                    nc.tensor.transpose(bank[:, g, u, :], pairs[:, block, plane], ident[:])
+            live["xT", n, block] = bank
+            if block == 0:
+                live["xg", n] = xg_pool.tile([P, PASSES, 4 * ROWS], BF16, name="xg", tag="xg",
+                                             align_bytes=64)
 
-        def copy_transposed(n, g, engine):
-            pairs = live["xg", n][:].bitcast(F32)
-            copy(engine, pairs[:, g, :].rearrange("p (i u) -> p i u", u=2),
-                 live["xT", n, g][:].rearrange("p u i -> p i u"))
+        def copy_transposed(n, block, engine):
+            pairs = live["xg", n][:].bitcast(F32)[:, :, 2 * block * P:2 * (block + 1) * P]
+            copy(engine, pairs.rearrange("p g (i u) -> p g i u", u=2),
+                 live["xT", n, block][:].rearrange("p g u i -> p g i u"))
+
+        def quantise_x_block(n, block):
+            for g in range(PASSES):
+                rows = slice(block * P, (block + 1) * P)
+                nc.vector.quantize_mx(out=x_codes[n][:, g, rows].bitcast(FP8X4),
+                                      scales=x_scales[n][:, g, rows],
+                                      in_=live["xg", n][:, g, 4 * block * P:4 * (block + 1) * P])
 
         def quantise_x(n):
             nc.vector.quantize_mx(out=x_codes[n][:].rearrange("p g i -> p (g i)").bitcast(FP8X4),
@@ -222,112 +231,155 @@ def tile_columncorrelationhead_kernel(tc, column_embeddings, W, b, out):
                                     op=ALU.max)
             nc.sync.dma_start(out=out_rows[:, BLOCKS * n:BLOCKS * (n + 1), :], in_=result[:])
 
-        load_x(0)
+        def quantise_xw_block(n, s, block):
+            if block == 0:
+                live["xwc", (n, s)] = (
+                    solo_pool.tile([P, ROWS], U32, name="xwc1", tag="xwc1", align_bytes=64),
+                    solo_pool.tile([P, ROWS], U8, name="xws1", tag="xws1", align_bytes=64))
+            codes, scales = live["xwc", (n, s)]
+            rows = slice(block * P, (block + 1) * P)
+            nc.vector.quantize_mx(out=codes[:, rows].bitcast(FP8X4), scales=scales[:, rows],
+                                  in_=live["xwg", (n, s)][:, rows, :].rearrange("p i t -> p (i t)"))
+
+        def second_matmul_block(n, block):
+            if block == 0:
+                live["o", n] = o_pool.tile([P, BLOCKS, ROWS], F32, name="o", tag="o")
+            bank = psum.tile([P, ROWS], F32, name="bank", tag="bank")
+            for s in range(PASSES):
+                key, place, batches = xw_place(n, s)
+                codes, scales = live["xwc", key]
+                rows = slice((BLOCKS * place + block) * P, (BLOCKS * place + block + 1) * P)
+                nc.tensor.matmul_mx(out=bank[:], lhsT=codes[:, rows].bitcast(FP8X4),
+                                    lhsT_scale=scales[:, rows],
+                                    rhs=x_codes[n][:, s, :].bitcast(FP8X4),
+                                    rhs_scale=x_scales[n][:, s, :],
+                                    start=(s == 0), stop=(s == PASSES - 1))
+            nc.scalar.activation(out=live["o", n][:, block, :], in_=bank[:], func=ACT.Tanh,
+                                 bias=bias[:, 0:1], scale=1.0)
+
+        def finish_block(n, block):
+            result = live["o", n]
+            diagonal = result[:, block, block * P:(block + 1) * P]
+            nc.vector.tensor_tensor(out=diagonal, in0=diagonal, in1=diag_mask[:], op=ALU.max)
+            nc.sync.dma_start(out=out_rows[:, BLOCKS * n + block, :], in_=result[:, block, :])
+
+        load_x_block(0, 0)
         load_w(0, 0)
         load_w(0, 1)
-        for n in range(1, 6):
+        load_x_block(0, 1)
+        for n in range(1, 4):
             load_x(n)
         load_w(1, 0)
+        load_x(4)
+        load_x(5)
         load_w(1, 1)
         for n in range(6, BATCHES):
             load_x(n)
 
-        warm_up(6)
-        transposes(0)
-        for group, engine in ((0, VECTOR), (1, VECTOR), (2, VECTOR), (3, SCALAR)):
-            regroup_w(0, 0, group, engine)
-        copy_transposed(0, 0, SCALAR)
-        copy_transposed(0, 1, SCALAR)
-        warm_up(5)
-        quantise_w(0, 0, 0, 2)
-        quantise_w(0, 0, 2, 2)
-        regroup_w(0, 1, 0, SCALAR)
-        regroup_w(0, 1, 1, VECTOR)
-        quantise_x(0)
-        transposes(1)
+        V, S = VECTOR, SCALAR
+        def both(n):
+            transposes(n, 0)
+            transposes(n, 1)
+        warm_up(3)
+        transposes(0, 0)
+        copy_transposed(0, 0, S)
+        regroup_w(0, 0, 0, V)
+        regroup_w(0, 0, 1, V)
+        regroup_w(0, 0, 3, S)
+        regroup_w(0, 0, 2, V)
+        quantise_x_block(0, 0)
+        warm_up(4)
+        regroup_w(0, 1, 0, V)
+        regroup_w(0, 1, 1, S)
+        quantise_w(0, 0, 0, GROUPS)
+        regroup_w(0, 1, 2, V)
         quantise_w(0, 1, 0, 2)
-        regroup_w(0, 1, 2, VECTOR)
-        regroup_w(0, 1, 3, SCALAR)
-        copy_transposed(1, 0, SCALAR)
+        regroup_w(0, 1, 3, S)
+        transposes(0, 1)
         first_matmul_open(0, 0, 0)
-        first_matmul_open(0, 0, 1)
+        copy_transposed(0, 1, S)
         quantise_w(0, 1, 2, 2)
+        quantise_x_block(0, 1)
+        first_matmul_close(0, 0, 0, S)
+        both(1)
+        sort_pairs(2, V)
+        copy_transposed(1, 0, V)
+        copy_transposed(1, 1, S)
         nc.vector.tensor_copy(out=bias[:], in_=b_bf16[:])
-        copy_transposed(1, 1, VECTOR)
+        first_matmul(0, 0, 1, S)
+        sort_pairs(3, V)
         quantise_x(1)
-        first_matmul_close(0, 0, 0, SCALAR)
-        first_matmul_close(0, 0, 1, VECTOR)
-
-        transposes(2)
-        copy_transposed(2, 0, SCALAR)
-        copy_transposed(2, 1, VECTOR)
+        both(2)
+        copy_transposed(2, 0, V)
+        copy_transposed(2, 1, S)
+        both(3)
+        copy_transposed(3, 0, V)
         quantise_x(2)
-        first_matmul(1, 0, 0, VECTOR)
-        first_matmul(1, 0, 1, VECTOR)
-        transposes(3)
-        first_matmul(2, 0, 0, SCALAR)
-        first_matmul(2, 0, 1, SCALAR)
-        copy_transposed(3, 0, VECTOR)
-        copy_transposed(3, 1, VECTOR)
-        transposes(4)
-        transposes(5)
-        copy_transposed(4, 1, SCALAR)
-        copy_transposed(5, 0, SCALAR)
+        copy_transposed(3, 1, S)
+        first_matmul(1, 0, 0, S)
         quantise_x(3)
-        copy_transposed(5, 1, SCALAR)
-        first_matmul(3, 0, 0, SCALAR)
-        regroup_w(1, 0, 1, VECTOR)
-        regroup_w(1, 0, 0, SCALAR)
-        copy_transposed(4, 0, VECTOR)
+        first_matmul(1, 0, 1, S)
+        regroup_w(1, 0, 0, V)
+        first_matmul(2, 0, 0, S)
+        regroup_w(1, 0, 1, V)
+        first_matmul(2, 0, 1, S)
+        both(4)
+        regroup_w(1, 0, 2, V)
+        regroup_w(1, 0, 3, S)
+        regroup_w(1, 1, 0, V)
+        copy_transposed(4, 0, V)
+        both(5)
+        regroup_w(1, 1, 1, V)
+        copy_transposed(4, 1, S)
+        copy_transposed(5, 0, V)
+        copy_transposed(5, 1, S)
         quantise_x(4)
-        first_matmul(3, 0, 1, SCALAR)
-        regroup_w(1, 0, 2, VECTOR)
+        regroup_w(1, 1, 2, V)
+        first_matmul(3, 0, 0, S)
         quantise_x(5)
-        first_matmul(4, 0, 0, SCALAR)
-        regroup_w(1, 0, 3, VECTOR)
-        first_matmul(4, 0, 1, SCALAR)
+        first_matmul(3, 0, 1, S)
         quantise_w(1, 0, 0, GROUPS)
-        regroup_w(1, 1, 0, VECTOR)
-        first_matmul(5, 0, 0, SCALAR)
-        first_matmul(5, 0, 1, SCALAR)
-        transposes(6)
-        transposes(7)
-        regroup_w(1, 1, 1, VECTOR)
-        regroup_w(1, 1, 2, VECTOR)
-        copy_transposed(6, 0, SCALAR)
-        regroup_w(1, 1, 3, VECTOR)
-        copy_transposed(7, 0, SCALAR)
+        regroup_w(1, 1, 3, V)
+        first_matmul(4, 0, 0, S)
+        first_matmul(4, 0, 1, S)
+        sort_pairs(6, V)
         quantise_w(1, 1, 0, GROUPS)
-        copy_transposed(7, 1, SCALAR)
-        copy_transposed(6, 1, VECTOR)
-
+        first_matmul(5, 0, 0, S)
+        first_matmul(5, 0, 1, S)
+        first_matmul(0, 1, 0, S)
+        first_matmul(0, 1, 1, V)
+        sort_pairs(7, V)
+        first_matmul(1, 1, 0, S)
+        first_matmul(1, 1, 1, S)
+        both(6)
+        both(7)
         quantise_xw(0, 0)
-        first_matmul(0, 1, 0, VECTOR)
+        copy_transposed(6, 0, V)
+        copy_transposed(6, 1, S)
         quantise_xw(2, 0)
-        first_matmul(0, 1, 1, SCALAR)
-        quantise_xw(4, 0)
-        first_matmul(1, 1, 0, SCALAR)
+        copy_transposed(7, 0, S)
+        copy_transposed(7, 1, V)
         quantise_x(6)
-        first_matmul(1, 1, 1, SCALAR)
+        quantise_xw(0, 1)
         quantise_x(7)
+        sort_pairs(8, V)
         for n in (2, 3):
             for block in range(BLOCKS):
-                first_matmul(n, 1, block, SCALAR)
-        quantise_xw(0, 1)
+                first_matmul(n, 1, block, S)
+        quantise_xw(4, 0)
         second_matmul(0)
+        sort_pairs(9, V)
         quantise_xw(2, 1)
         second_matmul(1)
-        first_matmul(4, 1, 0, SCALAR)
-        first_matmul(4, 1, 1, SCALAR)
+        first_matmul(4, 1, 0, S)
+        first_matmul(4, 1, 1, S)
         finish(0)
-        first_matmul(5, 1, 0, VECTOR)
-        first_matmul(5, 1, 1, SCALAR)
+        first_matmul(5, 1, 0, V)
+        first_matmul(5, 1, 1, S)
         second_matmul(2)
         quantise_xw(4, 1)
         finish(1)
         second_matmul(3)
-        sort_pairs(8)
-        sort_pairs(9)
 
         def pass_0(a):
             first_matmul(a, 0, 0, SCALAR)
@@ -343,8 +395,9 @@ def tile_columncorrelationhead_kernel(tc, column_embeddings, W, b, out):
             second_matmul(a - 2)
             quantise_xw(a, 0)
             second_matmul(a - 1)
-            transposes(a + 2)
-            transposes(a + 3)
+            for n in (a + 2, a + 3):
+                for block in range(BLOCKS):
+                    transposes(n, block)
             copy_transposed(a + 2, 0, VECTOR)
             copy_transposed(a + 2, 1, SCALAR)
             copy_transposed(a + 3, 0, SCALAR)
@@ -353,26 +406,33 @@ def tile_columncorrelationhead_kernel(tc, column_embeddings, W, b, out):
             first_matmul(a, 1, 0, SCALAR)
             first_matmul(a, 1, 1, SCALAR)
             if a + 4 < BATCHES:
-                sort_pairs(a + 4)
-                sort_pairs(a + 5)
+                sort_pairs(a + 4, VECTOR)
+                sort_pairs(a + 5, VECTOR)
             quantise_x(a + 3)
             first_matmul(a + 1, 1, 0, VECTOR)
             first_matmul(a + 1, 1, 1, SCALAR)
             quantise_xw(a, 1)
 
         pass_0(last)
+        second_matmul(last - 2)
         quantise_xw(last, 0)
         first_matmul(last, 1, 0, SCALAR)
         first_matmul(last, 1, 1, VECTOR)
+        finish(last - 2)
         first_matmul(last + 1, 1, 0, SCALAR)
         quantise_xw(last, 1)
         first_matmul(last + 1, 1, 1, VECTOR)
-        second_matmul(last - 2)
-        quantise_xw(last + 1, 1)
-        second_matmul(last - 1)
-        second_matmul(last)
-        finish(last - 2)
-        second_matmul(last + 1)
-        finish(last - 1)
-        finish(last)
-        finish(last + 1)
+        second_matmul_block(last - 1, 0)
+        second_matmul_block(last - 1, 1)
+        quantise_xw_block(last + 1, 1, 0)
+        quantise_xw_block(last + 1, 1, 1)
+        finish_block(last - 1, 0)
+        second_matmul_block(last, 0)
+        finish_block(last - 1, 1)
+        second_matmul_block(last, 1)
+        finish_block(last, 0)
+        second_matmul_block(last + 1, 0)
+        finish_block(last, 1)
+        second_matmul_block(last + 1, 1)
+        finish_block(last + 1, 0)
+        finish_block(last + 1, 1)

@@ -263,6 +263,27 @@ def tile_columncorrelationhead_kernel(tc, column_embeddings, W, b, out):
             nc.vector.tensor_tensor(out=diagonal, in0=diagonal, in1=diag_mask[:], op=ALU.max)
             nc.sync.dma_start(out=out_rows[:, BLOCKS * n + block, :], in_=result[:, block, :])
 
+        def first_matmul_wide(n, s, engines):
+            key, place, batches = xw_place(n, s)
+            if ("xwg", key) not in live:
+                live["xwg", key] = xwg_pool.tile([P, 2 * ROWS, 4], BF16, name="xwg", tag="xwg",
+                                                 align_bytes=64)
+            for half in range(2):
+                bank = psum.tile([P, 2, ROWS], F32, name="bank", tag="bank")
+                for v in range(2):
+                    t = 2 * half + v
+                    cols = slice(t * P, (t + 1) * P)
+                    for g in range(PASSES):
+                        nc.tensor.matmul_mx(out=bank[:, v, :],
+                                            lhsT=w_codes[s, g][:, cols].bitcast(FP8X4),
+                                            lhsT_scale=w_scales[s, g][:, cols],
+                                            rhs=x_codes[n][:, g, :].bitcast(FP8X4),
+                                            rhs_scale=x_scales[n][:, g, :],
+                                            start=(g == 0), stop=(g == PASSES - 1))
+                copy(engines[half], live["xwg", key][:, ROWS * place:ROWS * (place + 1),
+                                                     2 * half:2 * half + 2],
+                     bank[:].rearrange("p v i -> p i v"))
+
         load_x_block(0, 0)
         load_w(0, 0)
         load_w(0, 1)
@@ -382,12 +403,10 @@ def tile_columncorrelationhead_kernel(tc, column_embeddings, W, b, out):
         second_matmul(3)
 
         def pass_0(a):
-            first_matmul(a, 0, 0, SCALAR)
-            first_matmul(a, 0, 1, SCALAR)
+            first_matmul_wide(a, 0, (SCALAR, SCALAR))
             finish(a - 4)
-            first_matmul(a + 1, 0, 0, VECTOR)
+            first_matmul_wide(a + 1, 0, (VECTOR, SCALAR))
             finish(a - 3)
-            first_matmul(a + 1, 0, 1, SCALAR)
 
         last = BATCHES - 2
         for a in range(6, last, 2):
@@ -409,8 +428,7 @@ def tile_columncorrelationhead_kernel(tc, column_embeddings, W, b, out):
                 sort_pairs(a + 4, VECTOR)
                 sort_pairs(a + 5, VECTOR)
             quantise_x(a + 3)
-            first_matmul(a + 1, 1, 0, VECTOR)
-            first_matmul(a + 1, 1, 1, SCALAR)
+            first_matmul_wide(a + 1, 1, (VECTOR, SCALAR))
             quantise_xw(a, 1)
 
         pass_0(last)

@@ -411,9 +411,7 @@ def tile_columncorrelationhead_kernel(tc, column_embeddings, W, b, out):
         last = BATCHES - 2
         for a in range(6, last, 2):
             pass_0(a)
-            second_matmul(a - 2)
             quantise_xw(a, 0)
-            second_matmul(a - 1)
             for n in (a + 2, a + 3):
                 for block in range(BLOCKS):
                     transposes(n, block)
@@ -421,9 +419,10 @@ def tile_columncorrelationhead_kernel(tc, column_embeddings, W, b, out):
             copy_transposed(a + 2, 1, SCALAR)
             copy_transposed(a + 3, 0, SCALAR)
             copy_transposed(a + 3, 1, VECTOR)
+            second_matmul(a - 2)
             quantise_x(a + 2)
-            first_matmul(a, 1, 0, SCALAR)
-            first_matmul(a, 1, 1, SCALAR)
+            second_matmul(a - 1)
+            first_matmul_wide(a, 1, (SCALAR, SCALAR))
             if a + 4 < BATCHES:
                 sort_pairs(a + 4, VECTOR)
                 sort_pairs(a + 5, VECTOR)

@@ -363,8 +363,8 @@ def tile_columncorrelationhead_kernel(tc, column_embeddings, W, b, out):
         regroup_w(1, 1, 3, V)
         first_matmul(4, 0, 0, S)
         first_matmul(4, 0, 1, S)
-        sort_pairs(6, V)
         quantise_w(1, 1, 0, GROUPS)
+        sort_pairs(6, V)
         first_matmul(5, 0, 0, S)
         first_matmul(5, 0, 1, S)
         first_matmul(0, 1, 0, S)
@@ -392,8 +392,7 @@ def tile_columncorrelationhead_kernel(tc, column_embeddings, W, b, out):
         sort_pairs(9, V)
         quantise_xw(2, 1)
         second_matmul(1)
-        first_matmul(4, 1, 0, S)
-        first_matmul(4, 1, 1, S)
+        first_matmul_wide(4, 1, (S, S))
         finish(0)
         first_matmul(5, 1, 0, V)
         first_matmul(5, 1, 1, S)
@@ -422,12 +421,14 @@ def tile_columncorrelationhead_kernel(tc, column_embeddings, W, b, out):
             second_matmul(a - 2)
             quantise_x(a + 2)
             second_matmul(a - 1)
+            quantise_x(a + 3)
             first_matmul_wide(a, 1, (SCALAR, SCALAR))
             if a + 4 < BATCHES:
                 sort_pairs(a + 4, VECTOR)
+            first_matmul(a + 1, 1, 0, VECTOR)
+            first_matmul(a + 1, 1, 1, SCALAR)
+            if a + 4 < BATCHES:
                 sort_pairs(a + 5, VECTOR)
-            quantise_x(a + 3)
-            first_matmul_wide(a + 1, 1, (VECTOR, SCALAR))
             quantise_xw(a, 1)
 
         pass_0(last)

@@ -257,6 +257,29 @@ def tile_columncorrelationhead_kernel(tc, column_embeddings, W, b, out):
             nc.scalar.activation(out=live["o", n][:, block, :], in_=bank[:], func=ACT.Tanh,
                                  bias=bias[:, 0:1], scale=1.0)
 
+        def second_matmul_half(n, block, half):
+            bank = psum.tile([P, P], F32, name="bank", tag="bank")
+            cols = slice(half * P, (half + 1) * P)
+            for s in range(PASSES):
+                key, place, batches = xw_place(n, s)
+                codes, scales = live["xwc", key]
+                rows = slice((BLOCKS * place + block) * P, (BLOCKS * place + block + 1) * P)
+                nc.tensor.matmul_mx(out=bank[:], lhsT=codes[:, rows].bitcast(FP8X4),
+                                    lhsT_scale=scales[:, rows],
+                                    rhs=x_codes[n][:, s, cols].bitcast(FP8X4),
+                                    rhs_scale=x_scales[n][:, s, cols],
+                                    start=(s == 0), stop=(s == PASSES - 1))
+            nc.scalar.activation(out=live["o", n][:, block, cols], in_=bank[:], func=ACT.Tanh,
+                                 bias=bias[:, 0:1], scale=1.0)
+
+        def store_half(n, block, half):
+            cols = slice(half * P, (half + 1) * P)
+            nc.sync.dma_start(out=out_rows[:, BLOCKS * n + block, cols], in_=live["o", n][:, block, cols])
+
+        def diagonal_half(n, block):
+            diagonal = live["o", n][:, block, block * P:(block + 1) * P]
+            nc.vector.tensor_tensor(out=diagonal, in0=diagonal, in1=diag_mask[:], op=ALU.max)
+
         def finish_block(n, block):
             result = live["o", n]
             diagonal = result[:, block, block * P:(block + 1) * P]
@@ -307,51 +330,52 @@ def tile_columncorrelationhead_kernel(tc, column_embeddings, W, b, out):
         regroup_w(0, 0, 0, V)
         regroup_w(0, 0, 1, V)
         regroup_w(0, 0, 3, S)
-        regroup_w(0, 0, 2, V)
         quantise_x_block(0, 0)
+        quantise_w(0, 0, 0, 2)
         warm_up(4)
         regroup_w(0, 1, 0, V)
         regroup_w(0, 1, 1, S)
-        quantise_w(0, 0, 0, GROUPS)
-        regroup_w(0, 1, 2, V)
+        regroup_w(0, 0, 2, V)
         quantise_w(0, 1, 0, 2)
         regroup_w(0, 1, 3, S)
+        regroup_w(0, 1, 2, V)
         transposes(0, 1)
         first_matmul_open(0, 0, 0)
         copy_transposed(0, 1, S)
+        quantise_w(0, 0, 2, 2)
         quantise_w(0, 1, 2, 2)
-        quantise_x_block(0, 1)
-        first_matmul_close(0, 0, 0, S)
         both(1)
+        quantise_x_block(0, 1)
         sort_pairs(2, V)
-        copy_transposed(1, 0, V)
         copy_transposed(1, 1, S)
-        nc.vector.tensor_copy(out=bias[:], in_=b_bf16[:])
-        first_matmul(0, 0, 1, S)
+        copy_transposed(1, 0, V)
+        first_matmul_close(0, 0, 0, S)
         sort_pairs(3, V)
+        first_matmul(0, 0, 1, S)
+        nc.vector.tensor_copy(out=bias[:], in_=b_bf16[:])
         quantise_x(1)
         both(2)
         copy_transposed(2, 0, V)
         copy_transposed(2, 1, S)
         both(3)
-        copy_transposed(3, 0, V)
+        regroup_w(1, 0, 0, V)
         quantise_x(2)
         copy_transposed(3, 1, S)
+        copy_transposed(3, 0, V)
         first_matmul(1, 0, 0, S)
+        regroup_w(1, 0, 1, V)
         quantise_x(3)
         first_matmul(1, 0, 1, S)
-        regroup_w(1, 0, 0, V)
         first_matmul(2, 0, 0, S)
-        regroup_w(1, 0, 1, V)
+        regroup_w(1, 0, 2, V)
         first_matmul(2, 0, 1, S)
         both(4)
-        regroup_w(1, 0, 2, V)
         regroup_w(1, 0, 3, S)
         regroup_w(1, 1, 0, V)
         copy_transposed(4, 0, V)
         both(5)
-        regroup_w(1, 1, 1, V)
         copy_transposed(4, 1, S)
+        regroup_w(1, 1, 1, V)
         copy_transposed(5, 0, V)
         copy_transposed(5, 1, S)
         quantise_x(4)
@@ -359,8 +383,8 @@ def tile_columncorrelationhead_kernel(tc, column_embeddings, W, b, out):
         first_matmul(3, 0, 0, S)
         quantise_x(5)
         first_matmul(3, 0, 1, S)
-        quantise_w(1, 0, 0, GROUPS)
         regroup_w(1, 1, 3, V)
+        quantise_w(1, 0, 0, GROUPS)
         first_matmul(4, 0, 0, S)
         first_matmul(4, 0, 1, S)
         quantise_w(1, 1, 0, GROUPS)
@@ -368,8 +392,8 @@ def tile_columncorrelationhead_kernel(tc, column_embeddings, W, b, out):
         first_matmul(5, 0, 0, S)
         first_matmul(5, 0, 1, S)
         first_matmul(0, 1, 0, S)
-        first_matmul(0, 1, 1, V)
         sort_pairs(7, V)
+        first_matmul(0, 1, 1, V)
         first_matmul(1, 1, 0, S)
         first_matmul(1, 1, 1, S)
         both(6)
@@ -443,14 +467,17 @@ def tile_columncorrelationhead_kernel(tc, column_embeddings, W, b, out):
         second_matmul_block(last - 1, 0)
         second_matmul_block(last - 1, 1)
         quantise_xw_block(last + 1, 1, 0)
-        quantise_xw_block(last + 1, 1, 1)
         finish_block(last - 1, 0)
+        quantise_xw_block(last + 1, 1, 1)
         second_matmul_block(last, 0)
         finish_block(last - 1, 1)
         second_matmul_block(last, 1)
         finish_block(last, 0)
         second_matmul_block(last + 1, 0)
         finish_block(last, 1)
-        second_matmul_block(last + 1, 1)
+        second_matmul_half(last + 1, 1, 1)
         finish_block(last + 1, 0)
-        finish_block(last + 1, 1)
+        diagonal_half(last + 1, 1)
+        second_matmul_half(last + 1, 1, 0)
+        store_half(last + 1, 1, 1)
+        store_half(last + 1, 1, 0)

@@ -62,7 +62,6 @@ def tile_columncorrelationhead_kernel(tc, column_embeddings, W, b, out):
         nc.vector.tensor_scalar(out=diag_mask[:], in0=ident[:], scalar1=2.0, scalar2=-1.0,
                                 op0=ALU.mult, op1=ALU.add)
         b_bf16 = keep.tile([P, 1], BF16, name="b_bf16")
-        nc.scalar.dma_start(out=b_bf16[:], in_=b.partition_broadcast(P))
         table_load = keep.tile([P, 1], F32, name="table_load")
         nc.scalar.activation(out=table_load[:], in_=ident[:, 0:1], func=ACT.Tanh)
         bias = keep.tile([P, 1], F32, name="bias")
@@ -317,6 +316,7 @@ def tile_columncorrelationhead_kernel(tc, column_embeddings, W, b, out):
         load_x(4)
         load_x(5)
         load_w(1, 1)
+        nc.sync.dma_start(out=b_bf16[:], in_=b.partition_broadcast(P))
         for n in range(6, BATCHES):
             load_x(n)
 
@@ -352,7 +352,6 @@ def tile_columncorrelationhead_kernel(tc, column_embeddings, W, b, out):
         first_matmul_close(0, 0, 0, S)
         sort_pairs(3, V)
         first_matmul(0, 0, 1, S)
-        nc.vector.tensor_copy(out=bias[:], in_=b_bf16[:])
         quantise_x(1)
         both(2)
         copy_transposed(2, 0, V)
@@ -391,11 +390,9 @@ def tile_columncorrelationhead_kernel(tc, column_embeddings, W, b, out):
         sort_pairs(6, V)
         first_matmul(5, 0, 0, S)
         first_matmul(5, 0, 1, S)
-        first_matmul(0, 1, 0, S)
         sort_pairs(7, V)
-        first_matmul(0, 1, 1, V)
-        first_matmul(1, 1, 0, S)
-        first_matmul(1, 1, 1, S)
+        first_matmul_wide(0, 1, (S, V))
+        first_matmul_wide(1, 1, (S, S))
         both(6)
         both(7)
         quantise_xw(0, 0)
@@ -408,6 +405,7 @@ def tile_columncorrelationhead_kernel(tc, column_embeddings, W, b, out):
         quantise_xw(0, 1)
         quantise_x(7)
         sort_pairs(8, V)
+        nc.vector.tensor_copy(out=bias[:], in_=b_bf16[:])
         for n in (2, 3):
             for block in range(BLOCKS):
                 first_matmul(n, 1, block, S)

from contextlib import ExitStack

import concourse.mybir as mybir
from concourse.masks import make_identity

F32 = mybir.dt.float32
BF16 = mybir.dt.bfloat16
I32 = mybir.dt.int32
U32 = mybir.dt.uint32
U8 = mybir.dt.uint8
FP8X4 = mybir.dt.float8_e4m3fn_x4
ACT = mybir.ActivationFunctionType
ALU = mybir.AluOpType

P = 128
BATCHES, ROWS, FEATURES = 16, 256, 1024
PASS = 512
PASSES = FEATURES // PASS
GROUPS = 4
BLOCKS = ROWS // P
FLOPS = 2 * BATCHES * ROWS * FEATURES * FEATURES + 2 * BATCHES * ROWS * ROWS * FEATURES

VECTOR, SCALAR = "vector", "scalar"

QUANTISED_ALONE = ((14, 1), (15, 1))


def tile_columncorrelationhead_kernel(tc, column_embeddings, W, b, out):
    nc = tc.nc
    x_rows = column_embeddings.flatten_outer_dims().rearrange("(c p) d -> p c d", p=P)
    out_rows = out.flatten_outer_dims().rearrange("(c p) j -> p c j", p=P)
    w_view = W.rearrange("(g p t) c -> p g t c", g=PASSES, p=P, t=4)

    with ExitStack() as ctx:
        ctx.enter_context(tc.manual_schedule())
        keep = ctx.enter_context(tc.tile_pool(name="keep", bufs=1))
        xg_pool = ctx.enter_context(tc.tile_pool(name="xg_pool", bufs=4))
        xp_pool = ctx.enter_context(tc.tile_pool(name="xp_pool", bufs=5))
        xwg_pool = ctx.enter_context(tc.tile_pool(name="xwg_pool", bufs=4))
        xwc_pool = ctx.enter_context(tc.tile_pool(name="xwc_pool", bufs=6))
        solo_pool = ctx.enter_context(tc.tile_pool(name="solo_pool", bufs=2))
        o_pool = ctx.enter_context(tc.tile_pool(name="o_pool", bufs=6))
        psum = ctx.enter_context(tc.psum_pool(name="psum", bufs=8))

        def copy(engine, dst, src):
            if engine == VECTOR:
                nc.vector.tensor_copy(out=dst, in_=src)
            else:
                nc.scalar.copy(out=dst, in_=src)

        zero_codes = keep.tile([P, PASS], U32, name="zero_codes", align_bytes=64)
        zero_scales = keep.tile([P, PASS], U8, name="zero_scales", align_bytes=64)
        zeros = keep.tile([P, 2 * PASS], BF16, name="zeros", align_bytes=64)
        nc.vector.memset(zeros[:].bitcast(I32), 0)
        for half in range(2):
            cols = slice(half * PASS // 2, (half + 1) * PASS // 2)
            nc.vector.quantize_mx(out=zero_codes[:, cols].bitcast(FP8X4),
                                  scales=zero_scales[:, cols], in_=zeros[:])
        ident = keep.tile([P, P], F32, name="ident")
        make_identity(nc, ident[:])
        diag_mask = keep.tile([P, P], F32, name="diag_mask")
        nc.vector.tensor_scalar(out=diag_mask[:], in0=ident[:], scalar1=2.0, scalar2=-1.0,
                                op0=ALU.mult, op1=ALU.add)
        b_bf16 = keep.tile([P, 1], BF16, name="b_bf16")
        table_load = keep.tile([P, 1], F32, name="table_load")
        nc.scalar.activation(out=table_load[:], in_=ident[:, 0:1], func=ACT.Tanh)
        bias = keep.tile([P, 1], F32, name="bias")

        x_raw = [keep.tile([P, BLOCKS, FEATURES], BF16, name="x_raw%d" % n) for n in range(BATCHES)]
        x_codes = [keep.tile([P, PASSES, ROWS], U32, name="x_codes%d" % n, align_bytes=64)
                   for n in range(BATCHES)]
        x_scales = [keep.tile([P, PASSES, ROWS], U8, name="x_scales%d" % n, align_bytes=64)
                    for n in range(BATCHES)]
        w_raw, w_words, w_codes, w_scales = {}, {}, {}, {}
        for s in range(PASSES):
            for g in range(PASSES):
                w_raw[s, g] = keep.tile([P, 4, PASS], BF16, name="w_raw%d%d" % (s, g))
                w_words[s, g] = keep.tile([P, 4 * PASS], BF16, name="w_words%d%d" % (s, g),
                                          align_bytes=64)
                w_codes[s, g] = keep.tile([P, PASS], U32, name="w_codes%d%d" % (s, g),
                                          align_bytes=64)
                w_scales[s, g] = keep.tile([P, PASS], U8, name="w_scales%d%d" % (s, g),
                                           align_bytes=64)
        live = {}

        def load_x(n):
            nc.sync.dma_start(out=x_raw[n][:], in_=x_rows[:, BLOCKS * n:BLOCKS * (n + 1), :])

        def load_x_block(n, block):
            nc.sync.dma_start(out=x_raw[n][:, block, :], in_=x_rows[:, BLOCKS * n + block, :])

        def load_w(s, g):
            nc.sync.dma_start(out=w_raw[s, g][:], in_=w_view[:, g, :, s * PASS:(s + 1) * PASS])

        def warm_up(passes):
            scratch = psum.tile([P, PASS], F32, name="bank", tag="bank")
            for k in range(passes):
                nc.tensor.matmul_mx(out=scratch[:], lhsT=zero_codes[:, 0:P].bitcast(FP8X4),
                                    lhsT_scale=zero_scales[:, 0:P],
                                    rhs=zero_codes[:].bitcast(FP8X4), rhs_scale=zero_scales[:],
                                    start=True, stop=True)

        def sort_pairs(n, engine):
            live["xp", n] = xp_pool.tile([P, BLOCKS, FEATURES], BF16, name="xp", tag="xp",
                                         align_bytes=64)
            src = x_raw[n][:].bitcast(F32).rearrange("p b (g i u) -> p (b g) u i", g=PASSES, u=2)
            dst = live["xp", n][:].bitcast(F32).rearrange("p b (g u i) -> p (b g) u i", g=PASSES, u=2)
            copy(engine, dst, src)

        def transposes(n, block):
            is_sorted = ("xp", n) in live
            pairs = (live["xp", n] if is_sorted else x_raw[n])[:].bitcast(F32)
            bank = psum.tile([P, PASSES, 2, P], F32, name="bank", tag="bank")
            for g in range(PASSES):
                for u in range(2):
                    lo = (PASS // 2) * g
                    if is_sorted:
                        plane = slice(lo + u * P, lo + (u + 1) * P)
                    else:
                        plane = slice(lo + u, lo + PASS // 2, 2)
                    nc.tensor.transpose(bank[:, g, u, :], pairs[:, block, plane], ident[:])
            live["xT", n, block] = bank
            if block == 0:
                live["xg", n] = xg_pool.tile([P, PASSES, 4 * ROWS], BF16, name="xg", tag="xg",
                                             align_bytes=64)

        def copy_transposed(n, block, engine):
            pairs = live["xg", n][:].bitcast(F32)[:, :, 2 * block * P:2 * (block + 1) * P]
            copy(engine, pairs.rearrange("p g (i u) -> p g i u", u=2),
                 live["xT", n, block][:].rearrange("p g u i -> p g i u"))

        def quantise_x_block(n, block):
            for g in range(PASSES):
                rows = slice(block * P, (block + 1) * P)
                nc.vector.quantize_mx(out=x_codes[n][:, g, rows].bitcast(FP8X4),
                                      scales=x_scales[n][:, g, rows],
                                      in_=live["xg", n][:, g, 4 * block * P:4 * (block + 1) * P])

        def quantise_x(n):
            nc.vector.quantize_mx(out=x_codes[n][:].rearrange("p g i -> p (g i)").bitcast(FP8X4),
                                  scales=x_scales[n][:].rearrange("p g i -> p (g i)"),
                                  in_=live["xg", n][:].rearrange("p g c -> p (g c)"))

        def regroup_w(s, g, group, engine):
            src = w_raw[s, g][:].rearrange("p t (q f) -> p f q t", f=GROUPS)[:, group]
            dst = w_words[s, g][:].rearrange("p (f q t) -> p f q t", f=GROUPS, t=4)[:, group]
            copy(engine, dst, src)

        def quantise_w(s, g, first_group, groups):
            words = slice(first_group * P, (first_group + groups) * P)
            nc.vector.quantize_mx(out=w_codes[s, g][:, words].bitcast(FP8X4),
                                  scales=w_scales[s, g][:, words],
                                  in_=w_words[s, g][:, 4 * first_group * P:4 * (first_group + groups) * P])

        def first_matmul_groups(n, s, block, groups):
            bank = live["xwT", n, s, block]
            rows = slice(block * P, (block + 1) * P)
            for t in groups:
                cols = slice(t * P, (t + 1) * P)
                for g in range(PASSES):
                    nc.tensor.matmul_mx(out=bank[:, cols],
                                        lhsT=w_codes[s, g][:, cols].bitcast(FP8X4),
                                        lhsT_scale=w_scales[s, g][:, cols],
                                        rhs=x_codes[n][:, g, rows].bitcast(FP8X4),
                                        rhs_scale=x_scales[n][:, g, rows],
                                        start=(g == 0), stop=(g == PASSES - 1))

        def first_matmul_open(n, s, block):
            live["xwT", n, s, block] = psum.tile([P, PASS], F32, name="bank", tag="bank")
            first_matmul_groups(n, s, block, (0, 1))

        def xw_place(n, s):
            if (n, s) in QUANTISED_ALONE:
                return (n, s), 0, 1
            return (n - n % 2, s), n % 2, 2

        def first_matmul_close(n, s, block, engine):
            first_matmul_groups(n, s, block, (2, 3))
            key, place, batches = xw_place(n, s)
            if ("xwg", key) not in live:
                if batches == 1:
                    live["xwg", key] = solo_pool.tile([P, ROWS, 4], BF16, name="xwg1", tag="xwg1",
                                                      align_bytes=64)
                else:
                    live["xwg", key] = xwg_pool.tile([P, 2 * ROWS, 4], BF16, name="xwg", tag="xwg",
                                                     align_bytes=64)
            lo = (BLOCKS * place + block) * P
            copy(engine, live["xwg", key][:, lo:lo + P, :],
                 live["xwT", n, s, block][:].rearrange("p (t i) -> p i t", t=GROUPS))

        def first_matmul(n, s, block, engine):
            first_matmul_open(n, s, block)
            first_matmul_close(n, s, block, engine)

        def quantise_xw(n, s):
            key, place, batches = xw_place(n, s)
            if batches == 1:
                codes = solo_pool.tile([P, ROWS], U32, name="xwc1", tag="xwc1", align_bytes=64)
                scales = solo_pool.tile([P, ROWS], U8, name="xws1", tag="xws1", align_bytes=64)
            else:
                codes = xwc_pool.tile([P, 2 * ROWS], U32, name="xwc", tag="xwc", align_bytes=64)
                scales = xwc_pool.tile([P, 2 * ROWS], U8, name="xws", tag="xws", align_bytes=64)
            nc.vector.quantize_mx(out=codes[:].bitcast(FP8X4), scales=scales[:],
                                  in_=live["xwg", key][:].rearrange("p i t -> p (i t)"))
            live["xwc", key] = (codes, scales)

        def second_matmul(n):
            result = o_pool.tile([P, BLOCKS, ROWS], F32, name="o", tag="o")
            live["o", n] = result
            bank = psum.tile([P, PASS], F32, name="bank", tag="bank")
            for block in range(BLOCKS):
                for s in range(PASSES):
                    key, place, batches = xw_place(n, s)
                    codes, scales = live["xwc", key]
                    rows = slice((BLOCKS * place + block) * P, (BLOCKS * place + block + 1) * P)
                    nc.tensor.matmul_mx(out=bank[:, block * ROWS:(block + 1) * ROWS],
                                        lhsT=codes[:, rows].bitcast(FP8X4),
                                        lhsT_scale=scales[:, rows],
                                        rhs=x_codes[n][:, s, :].bitcast(FP8X4),
                                        rhs_scale=x_scales[n][:, s, :],
                                        start=(s == 0), stop=(s == PASSES - 1))
            nc.scalar.activation(out=result[:], in_=bank[:].rearrange("p (r j) -> p r j", r=BLOCKS),
                                 func=ACT.Tanh, bias=bias[:, 0:1], scale=1.0)

        def finish(n):
            result = live["o", n]
            diagonal = result[:].rearrange("p r (a k) -> p (r a) k", k=P)[:, 0:4:3, :]
            nc.vector.tensor_tensor(out=diagonal, in0=diagonal,
                                    in1=diag_mask[:].unsqueeze(1).to_broadcast([P, BLOCKS, P]),
                                    op=ALU.max)
            nc.sync.dma_start(out=out_rows[:, BLOCKS * n:BLOCKS * (n + 1), :], in_=result[:])

        def quantise_xw_block(n, s, block):
            if block == 0:
                live["xwc", (n, s)] = (
                    solo_pool.tile([P, ROWS], U32, name="xwc1", tag="xwc1", align_bytes=64),
                    solo_pool.tile([P, ROWS], U8, name="xws1", tag="xws1", align_bytes=64))
            codes, scales = live["xwc", (n, s)]
            rows = slice(block * P, (block + 1) * P)
            nc.vector.quantize_mx(out=codes[:, rows].bitcast(FP8X4), scales=scales[:, rows],
                                  in_=live["xwg", (n, s)][:, rows, :].rearrange("p i t -> p (i t)"))

        def second_matmul_block(n, block):
            if block == 0:
                live["o", n] = o_pool.tile([P, BLOCKS, ROWS], F32, name="o", tag="o")
            bank = psum.tile([P, ROWS], F32, name="bank", tag="bank")
            for s in range(PASSES):
                key, place, batches = xw_place(n, s)
                codes, scales = live["xwc", key]
                rows = slice((BLOCKS * place + block) * P, (BLOCKS * place + block + 1) * P)
                nc.tensor.matmul_mx(out=bank[:], lhsT=codes[:, rows].bitcast(FP8X4),
                                    lhsT_scale=scales[:, rows],
                                    rhs=x_codes[n][:, s, :].bitcast(FP8X4),
                                    rhs_scale=x_scales[n][:, s, :],
                                    start=(s == 0), stop=(s == PASSES - 1))
            nc.scalar.activation(out=live["o", n][:, block, :], in_=bank[:], func=ACT.Tanh,
                                 bias=bias[:, 0:1], scale=1.0)

        def second_matmul_half(n, block, half):
            bank = psum.tile([P, P], F32, name="bank", tag="bank")
            cols = slice(half * P, (half + 1) * P)
            for s in range(PASSES):
                key, place, batches = xw_place(n, s)
                codes, scales = live["xwc", key]
                rows = slice((BLOCKS * place + block) * P, (BLOCKS * place + block + 1) * P)
                nc.tensor.matmul_mx(out=bank[:], lhsT=codes[:, rows].bitcast(FP8X4),
                                    lhsT_scale=scales[:, rows],
                                    rhs=x_codes[n][:, s, cols].bitcast(FP8X4),
                                    rhs_scale=x_scales[n][:, s, cols],
                                    start=(s == 0), stop=(s == PASSES - 1))
            nc.scalar.activation(out=live["o", n][:, block, cols], in_=bank[:], func=ACT.Tanh,
                                 bias=bias[:, 0:1], scale=1.0)

        def store_half(n, block, half):
            cols = slice(half * P, (half + 1) * P)
            nc.sync.dma_start(out=out_rows[:, BLOCKS * n + block, cols], in_=live["o", n][:, block, cols])

        def diagonal_half(n, block):
            diagonal = live["o", n][:, block, block * P:(block + 1) * P]
            nc.vector.tensor_tensor(out=diagonal, in0=diagonal, in1=diag_mask[:], op=ALU.max)

        def finish_block(n, block):
            result = live["o", n]
            diagonal = result[:, block, block * P:(block + 1) * P]
            nc.vector.tensor_tensor(out=diagonal, in0=diagonal, in1=diag_mask[:], op=ALU.max)
            nc.sync.dma_start(out=out_rows[:, BLOCKS * n + block, :], in_=result[:, block, :])

        def first_matmul_wide(n, s, engines):
            key, place, batches = xw_place(n, s)
            if ("xwg", key) not in live:
                live["xwg", key] = xwg_pool.tile([P, 2 * ROWS, 4], BF16, name="xwg", tag="xwg",
                                                 align_bytes=64)
            for half in range(2):
                bank = psum.tile([P, 2, ROWS], F32, name="bank", tag="bank")
                for v in range(2):
                    t = 2 * half + v
                    cols = slice(t * P, (t + 1) * P)
                    for g in range(PASSES):
                        nc.tensor.matmul_mx(out=bank[:, v, :],
                                            lhsT=w_codes[s, g][:, cols].bitcast(FP8X4),
                                            lhsT_scale=w_scales[s, g][:, cols],
                                            rhs=x_codes[n][:, g, :].bitcast(FP8X4),
                                            rhs_scale=x_scales[n][:, g, :],
                                            start=(g == 0), stop=(g == PASSES - 1))
                copy(engines[half], live["xwg", key][:, ROWS * place:ROWS * (place + 1),
                                                     2 * half:2 * half + 2],
                     bank[:].rearrange("p v i -> p i v"))

        load_x_block(0, 0)
        load_w(0, 0)
        load_w(0, 1)
        load_x_block(0, 1)
        for n in range(1, 4):
            load_x(n)
        load_w(1, 0)
        load_x(4)
        load_x(5)
        load_w(1, 1)
        nc.sync.dma_start(out=b_bf16[:], in_=b.partition_broadcast(P))
        for n in range(6, BATCHES):
            load_x(n)

        V, S = VECTOR, SCALAR
        def both(n):
            transposes(n, 0)
            transposes(n, 1)
        warm_up(3)
        transposes(0, 0)
        copy_transposed(0, 0, S)
        regroup_w(0, 0, 0, V)
        regroup_w(0, 0, 1, V)
        regroup_w(0, 0, 3, S)
        quantise_x_block(0, 0)
        quantise_w(0, 0, 0, 2)
        warm_up(4)
        regroup_w(0, 1, 0, V)
        regroup_w(0, 1, 1, S)
        regroup_w(0, 0, 2, V)
        quantise_w(0, 1, 0, 2)
        regroup_w(0, 1, 3, S)
        regroup_w(0, 1, 2, V)
        transposes(0, 1)
        first_matmul_open(0, 0, 0)
        copy_transposed(0, 1, S)
        quantise_w(0, 0, 2, 2)
        quantise_w(0, 1, 2, 2)
        both(1)
        quantise_x_block(0, 1)
        sort_pairs(2, V)
        copy_transposed(1, 1, S)
        copy_transposed(1, 0, V)
        first_matmul_close(0, 0, 0, S)
        sort_pairs(3, V)
        first_matmul(0, 0, 1, S)
        quantise_x(1)
        both(2)
        copy_transposed(2, 0, V)
        copy_transposed(2, 1, S)
        both(3)
        regroup_w(1, 0, 0, V)
        quantise_x(2)
        copy_transposed(3, 1, S)
        copy_transposed(3, 0, V)
        first_matmul(1, 0, 0, S)
        regroup_w(1, 0, 1, V)
        quantise_x(3)
        first_matmul(1, 0, 1, S)
        first_matmul(2, 0, 0, S)
        regroup_w(1, 0, 2, V)
        first_matmul(2, 0, 1, S)
        both(4)
        regroup_w(1, 0, 3, S)
        regroup_w(1, 1, 0, V)
        copy_transposed(4, 0, V)
        both(5)
        copy_transposed(4, 1, S)
        regroup_w(1, 1, 1, V)
        copy_transposed(5, 0, V)
        copy_transposed(5, 1, S)
        quantise_x(4)
        regroup_w(1, 1, 2, V)
        first_matmul(3, 0, 0, S)
        quantise_x(5)
        first_matmul(3, 0, 1, S)
        regroup_w(1, 1, 3, V)
        quantise_w(1, 0, 0, GROUPS)
        first_matmul(4, 0, 0, S)
        first_matmul(4, 0, 1, S)
        quantise_w(1, 1, 0, GROUPS)
        sort_pairs(6, V)
        first_matmul(5, 0, 0, S)
        first_matmul(5, 0, 1, S)
        sort_pairs(7, V)
        first_matmul_wide(0, 1, (S, V))
        first_matmul_wide(1, 1, (S, S))
        both(6)
        both(7)
        quantise_xw(0, 0)
        copy_transposed(6, 0, V)
        copy_transposed(6, 1, S)
        quantise_xw(2, 0)
        copy_transposed(7, 0, S)
        copy_transposed(7, 1, V)
        quantise_x(6)
        quantise_xw(0, 1)
        quantise_x(7)
        sort_pairs(8, V)
        nc.vector.tensor_copy(out=bias[:], in_=b_bf16[:])
        for n in (2, 3):
            for block in range(BLOCKS):
                first_matmul(n, 1, block, S)
        quantise_xw(4, 0)
        second_matmul(0)
        sort_pairs(9, V)
        quantise_xw(2, 1)
        second_matmul(1)
        first_matmul_wide(4, 1, (S, S))
        finish(0)
        first_matmul(5, 1, 0, V)
        first_matmul(5, 1, 1, S)
        second_matmul(2)
        quantise_xw(4, 1)
        finish(1)
        second_matmul(3)

        def pass_0(a):
            first_matmul_wide(a, 0, (SCALAR, SCALAR))
            finish(a - 4)
            first_matmul_wide(a + 1, 0, (VECTOR, SCALAR))
            finish(a - 3)

        last = BATCHES - 2
        for a in range(6, last, 2):
            pass_0(a)
            quantise_xw(a, 0)
            for n in (a + 2, a + 3):
                for block in range(BLOCKS):
                    transposes(n, block)
            copy_transposed(a + 2, 0, VECTOR)
            copy_transposed(a + 2, 1, SCALAR)
            copy_transposed(a + 3, 0, SCALAR)
            copy_transposed(a + 3, 1, VECTOR)
            second_matmul(a - 2)
            quantise_x(a + 2)
            second_matmul(a - 1)
            quantise_x(a + 3)
            first_matmul_wide(a, 1, (SCALAR, SCALAR))
            if a + 4 < BATCHES:
                sort_pairs(a + 4, VECTOR)
            first_matmul(a + 1, 1, 0, VECTOR)
            first_matmul(a + 1, 1, 1, SCALAR)
            if a + 4 < BATCHES:
                sort_pairs(a + 5, VECTOR)
            quantise_xw(a, 1)

        pass_0(last)
        second_matmul(last - 2)
        quantise_xw(last, 0)
        first_matmul(last, 1, 0, SCALAR)
        first_matmul(last, 1, 1, VECTOR)
        finish(last - 2)
        first_matmul(last + 1, 1, 0, SCALAR)
        quantise_xw(last, 1)
        first_matmul(last + 1, 1, 1, VECTOR)
        second_matmul_block(last - 1, 0)
        second_matmul_block(last - 1, 1)
        quantise_xw_block(last + 1, 1, 0)
        finish_block(last - 1, 0)
        quantise_xw_block(last + 1, 1, 1)
        second_matmul_block(last, 0)
        finish_block(last - 1, 1)
        second_matmul_block(last, 1)
        finish_block(last, 0)
        second_matmul_block(last + 1, 0)
        finish_block(last, 1)
        second_matmul_half(last + 1, 1, 1)
        finish_block(last + 1, 0)
        diagonal_half(last + 1, 1)
        second_matmul_half(last + 1, 1, 0)
        store_half(last + 1, 1, 1)
        store_half(last + 1, 1, 0)
